import numpy as np
import ml_dtypes


def mxq(x, axis, fmt="e4m3"):
    dtype, down = {"e4m3": (ml_dtypes.float8_e4m3fn, 7), "e5m2": (ml_dtypes.float8_e5m2, 14)}[fmt]
    v = np.moveaxis(np.asarray(x, np.float32).astype(ml_dtypes.bfloat16).astype(np.float64), axis, -1)
    blocks = v.reshape(v.shape[:-1] + (-1, 32))
    amax = np.abs(blocks).max(-1, keepdims=True)
    byte = np.maximum(np.where(amax > 0, np.frexp(amax)[1] - 1 + 127, 0) - down, 1)
    scale = np.exp2(byte - 127.0)
    codes = (blocks / scale).astype(np.float32).astype(dtype).astype(np.float64)
    return np.moveaxis((codes * scale).reshape(v.shape), -1, axis)


WIDE = False


def mx_kscale(k):
    if not WIDE:
        return np.ones(k)
    levels = np.array([10, -10, 5, -5, 0])
    if k % 512:
        return np.exp2(np.random.permutation(np.resize(levels, k // 32))).repeat(32)
    a = np.empty((k // 512, 16))
    for p in range(k // 512):
        a[p, :8] = np.random.permutation(np.resize(levels, 8))
        for g in range(8):
            far = levels[np.abs(levels - a[p, g]) >= 10]
            a[p, g + 8] = far[np.random.randint(len(far))]
    return np.exp2(a.ravel()).repeat(32)


BF16 = ml_dtypes.bfloat16


def bf(x):
    return np.asarray(x, np.float32).astype(BF16)


def f64(x):
    return np.asarray(x).astype(np.float64)


B, HC, WC, C, F = 128, 8, 4, 512, 128


def setup_inputs():
    s = mx_kscale(C)
    x_crop = np.stack([np.random.standard_normal((B, HC, WC, C)), np.random.standard_normal((B, HC, WC, C))], axis=1)
    return {"x_crop": bf(x_crop * s),
            "W_r": bf(np.random.standard_normal((HC, WC, C, F)) * 0.5 / np.sqrt(C) / s[:, None]),
            "W_i": bf(np.random.standard_normal((HC, WC, C, F)) * 0.5 / np.sqrt(C) / s[:, None]),
            "b_r": bf(np.random.standard_normal(F) * 0.3),
            "b_i": bf(np.random.standard_normal(F) * 0.3)}


def core(x_crop, W_r, W_i, b_r, b_i):
    sp = f64(x_crop)
    xr = mxq(sp[:, 0].transpose(1, 2, 0, 3), 3, "e4m3")
    xi = mxq(sp[:, 1].transpose(1, 2, 0, 3), 3, "e4m3")
    wr = mxq(f64(W_r), 2, "e4m3")
    wi = mxq(f64(W_i), 2, "e4m3")
    rr = xr @ wr
    ii = xi @ wi
    ri = xr @ wi
    ir = xi @ wr
    r = rr - ii + f64(b_r)
    i = ri + ir + f64(b_i)
    y = np.stack([r.transpose(2, 0, 1, 3), i.transpose(2, 0, 1, 3)], axis=1)
    return np.maximum(y, 0.0)


def e4m3fn_bytes(y):
    return np.clip(np.asarray(y, np.float64), -448.0, 448.0).astype(np.float32).astype(ml_dtypes.float8_e4m3fn).view(np.uint8)


def reference(x_crop, W_r, W_i, b_r, b_i):
    out = core(x_crop, W_r, W_i, b_r, b_i)
    s = np.max(np.abs(out), axis=-1, keepdims=True) / 448.0
    return out, e4m3fn_bytes(out / s)

@@ -1,0 +1,354 @@
+from contextlib import ExitStack
+
+import concourse.mybir as mybir
+from concourse.masks import make_identity
+
+F32 = mybir.dt.float32
+BF16 = mybir.dt.bfloat16
+U32 = mybir.dt.uint32
+U8 = mybir.dt.uint8
+FP8X4 = mybir.dt.float8_e4m3fn_x4
+FP8 = mybir.dt.float8_e4m3fn
+ALU = mybir.AluOpType
+ACT = mybir.ActivationFunctionType
+AX = mybir.AxisListType
+
+P = 128
+B, PIX, C, F = 128, 32, 512, 128
+GMAX = 4
+
+FLOPS = 4 * PIX * 2 * B * C * F
+
+GROUPS = [2,2,2,2,4,4,4,4,4,2,2]
+X_CHUNKS = [2,2,2,2,4,4,4,4,4,2,2]
+RES_CHUNKS = [8,8,8,4,2,2]
+BYTE_CHUNKS = [16,8,4,2,2]
+V_SLICES = [2,0,0,0,0,0,0,0,0,0,0]
+G_SLICES = [0,2,2,2,4,4,4,4,4,2,2]
+V_BANKS = [0,0,0,0,1,1,1,1,1,0,0]
+V_CASTS = [0,0,0,0,0,0,0,0,0,0,2]
+LOADS_AHEAD = 3
+BLOCKED = "vs"
+ORDER = "H"
+
+
+def starts(sizes):
+    return [sum(sizes[:c]) for c in range(len(sizes))]
+
+
+def chunk_of(sizes, pixel):
+    for c, s in enumerate(starts(sizes)):
+        if s <= pixel < s + sizes[c]:
+            return c, pixel - s
+    raise ValueError("pixel out of range")
+
+
+def tile_dot_pa_kernel(tc, x_crop, W_r, W_i, b_r, b_i, out_0, out_1):
+    nc = tc.nc
+    x = x_crop.rearrange("b r h w c -> b r (h w) c")
+    w_dram = [
+        W_r.rearrange("h w (p j) f -> p (h w) j f", j=4),
+        W_i.rearrange("h w (p j) f -> p (h w) j f", j=4),
+    ]
+    o0 = out_0.rearrange("b r h w f -> b r (h w) f")
+    o1 = out_1.rearrange("b r h w f -> b r (h w) f")
+    N = len(GROUPS)
+    first = starts(GROUPS)
+    assert sum(GROUPS) == PIX and sum(X_CHUNKS) == PIX and sum(RES_CHUNKS) == PIX and sum(BYTE_CHUNKS) == PIX
+
+    with ExitStack() as ctx:
+        const = ctx.enter_context(tc.tile_pool(name="const", bufs=1))
+        raw = ctx.enter_context(tc.tile_pool(name="raw", bufs=1))
+        grp = ctx.enter_context(tc.tile_pool(name="grp", bufs=2))
+        code = ctx.enter_context(tc.tile_pool(name="code", bufs=2))
+        epi = ctx.enter_context(tc.tile_pool(name="epi", bufs=2))
+        sml = ctx.enter_context(tc.tile_pool(name="sml", bufs=3))
+        pt = ctx.enter_context(tc.psum_pool(name="pt", bufs=5))
+        pa = ctx.enter_context(tc.psum_pool(name="pa", bufs=1))
+        ctx.enter_context(tc.manual_schedule())
+
+        st = {}
+
+        def pixels(g):
+            return slice(first[g], first[g] + GROUPS[g])
+
+        def load(g):
+            if g < 0 or g >= N:
+                return
+            n = GROUPS[g]
+            c, off = chunk_of(X_CHUNKS, first[g])
+            if off == 0:
+                m = X_CHUNKS[c]
+                xr = raw.tile([P, 2, m, C], BF16, name="x_raw%d" % c)
+                nc.sync.dma_start(out=xr[:], in_=x[:, :, first[g] : first[g] + m, :])
+                st["x_raw", c] = xr
+            wr = raw.tile([P, 2, n, 4, F], BF16, name="w_raw%d" % g)
+            nc.sync.dma_start(out=wr[:, 0], in_=w_dram[0][:, pixels(g)])
+            nc.sync.dma_start(out=wr[:, 1], in_=w_dram[1][:, pixels(g)])
+            st["w_raw", g] = wr
+
+        def transposes(g):
+            if g < 0 or g >= N:
+                return
+            n = GROUPS[g]
+            c, off = chunk_of(X_CHUNKS, first[g])
+            m = X_CHUNKS[c]
+            words = st["x_raw", c][:].rearrange("b r q c -> b (r q c)").bitcast(F32)
+            banks = []
+            for h in range(n):
+                xt = pt.tile([P, 2, 2, B], F32, name="xt", tag="xt")
+                for i in range(2):
+                    s = 2 * h + i
+                    row = (s // n) * m + off + s % n
+                    for u in range(2):
+                        nc.tensor.transpose(xt[:, i, u, :], words[:, 256 * row + u : 256 * (row + 1) : 2], ident[:])
+                banks.append(xt)
+            st["xt", g] = banks
+
+        def x_alloc(g):
+            if g < 0 or g >= N:
+                return
+            st["xg", g] = grp.tile([P, 2 * GROUPS[g], B, 4], BF16, name="xg", tag="xg", align_bytes=64)
+
+        def x_copies(g, eng):
+            if g < 0 or g >= N:
+                return
+            n = GROUPS[g]
+            xg_w = st["xg", g][:].rearrange("p s b t -> p (s b t)").bitcast(F32).rearrange("p (s b u) -> p s b u", s=2 * n, u=2)
+            for h in range(n):
+                src = st["xt", g][h][:].rearrange("p i u b -> p i b u")
+                on_v = h >= n - V_BANKS[g]
+                if on_v and eng == "v":
+                    nc.vector.tensor_copy(out=xg_w[:, 2 * h : 2 * h + 2], in_=src)
+                if not on_v and eng == "s":
+                    nc.scalar.copy(out=xg_w[:, 2 * h : 2 * h + 2], in_=src)
+
+        def w_alloc(g):
+            if g < 0 or g >= N:
+                return
+            st["wg", g] = grp.tile([P, 2 * GROUPS[g], F, 4], BF16, name="wg", tag="wg", align_bytes=64, bufs=1)
+
+        def w_interleave(g, part):
+            if g < 0 or g >= N:
+                return
+            n = GROUPS[g]
+            a = V_SLICES[g]
+            e = a + G_SLICES[g]
+            h = a // 2 if a >= 4 else a
+            lo, hi = {"v0": (0, h), "v1": (h, a), "g": (a, e), "s": (e, 2 * n)}[part]
+            if hi <= lo:
+                return
+            wg = st["wg", g]
+            w_src = st["w_raw", g][:].rearrange("p w q j f -> p (w q) f j")
+            blk_dst = wg[:, lo:hi].rearrange("p s (c i) j -> p s c j i", i=4)
+            blk_src = st["w_raw", g][:].rearrange("p w q j f -> p (w q) j f")[:, lo:hi].rearrange("p s j (c i) -> p s c j i", i=4)
+            if part == "s" and "s" in BLOCKED:
+                nc.scalar.copy(out=blk_dst, in_=blk_src)
+            elif part in ("v0", "v1") and "v" in BLOCKED:
+                nc.vector.tensor_copy(out=blk_dst, in_=blk_src)
+            elif part == "s":
+                nc.scalar.copy(out=wg[:, lo:hi], in_=w_src[:, lo:hi])
+            elif part == "g":
+                nc.gpsimd.tensor_scalar(out=wg[:, lo:hi], in0=w_src[:, lo:hi], scalar1=1.0, scalar2=0.0, op0=ALU.mult, op1=ALU.add)
+            else:
+                nc.vector.tensor_copy(out=wg[:, lo:hi], in_=w_src[:, lo:hi])
+
+        def quant_x(g):
+            if g < 0 or g >= N:
+                return
+            n = GROUPS[g]
+            xc = code.tile([P, 2 * n * B], U32, name="xc", tag="xc", align_bytes=64)
+            xs = code.tile([P, 2 * n * B], U8, name="xs", tag="xs", align_bytes=64)
+            nc.vector.quantize_mx(out=xc[:].bitcast(FP8X4), scales=xs[:], in_=st["xg", g][:].rearrange("p s b t -> p (s b t)"))
+            st["qx", g] = (xc, xs)
+
+        def quant_w(g):
+            if g < 0 or g >= N:
+                return
+            n = GROUPS[g]
+            wc = code.tile([P, 2 * n * F], U32, name="wc", tag="wc", align_bytes=64)
+            ws = code.tile([P, 2 * n * F], U8, name="ws", tag="ws", align_bytes=64)
+            nc.vector.quantize_mx(out=wc[:].bitcast(FP8X4), scales=ws[:], in_=st["wg", g][:].rearrange("p s f t -> p (s f t)"))
+            st["qw", g] = (wc, ws)
+
+        def products(g):
+            if g < 0 or g >= N:
+                return
+            n = GROUPS[g]
+            xc, xs = st["qx", g]
+            wc, ws = st["qw", g]
+            acc_rr = pa.tile([P, n, F], F32, name="acc_rr", tag="acc_rr")
+            acc_ii = pa.tile([P, n, F], F32, name="acc_ii", tag="acc_ii")
+            acc_im = pa.tile([P, n, F], F32, name="acc_im", tag="acc_im")
+
+            def mm(out, sx, sw, start, stop):
+                cx = slice(B * sx, B * (sx + 1))
+                cw = slice(F * sw, F * (sw + 1))
+                nc.tensor.matmul_mx(
+                    out=out,
+                    lhsT=xc[:, cx].bitcast(FP8X4),
+                    lhsT_scale=xs[:, cx],
+                    rhs=wc[:, cw].bitcast(FP8X4),
+                    rhs_scale=ws[:, cw],
+                    start=start,
+                    stop=stop,
+                )
+
+            for q in range(n):
+                mm(acc_ii[:, q, :], n + q, n + q, True, True)
+            for q in range(n):
+                mm(acc_im[:, q, :], n + q, q, True, False)
+                mm(acc_im[:, q, :], q, n + q, False, True)
+            for q in range(n):
+                mm(acc_rr[:, q, :], q, q, True, True)
+            st["acc", g] = (acc_rr, acc_ii, acc_im)
+
+        def sums(g):
+            if g < 0 or g >= N:
+                return
+            n = GROUPS[g]
+            acc_rr, acc_ii, acc_im = st["acc", g]
+            t = epi.tile([P, n, F], F32, name="t", tag="t")
+            y = epi.tile([P, 2, n, F], F32, name="y", tag="y")
+            nc.vector.scalar_tensor_tensor(
+                out=t[:],
+                in0=acc_ii[:],
+                scalar=-1.0,
+                in1=bias[:, 0:1, :].to_broadcast([P, n, F]),
+                op0=ALU.mult,
+                op1=ALU.add,
+            )
+            nc.vector.tensor_tensor(out=y[:, 1], in0=acc_im[:], in1=bias[:, 1:2, :].to_broadcast([P, n, F]), op=ALU.add)
+            nc.vector.tensor_tensor(out=y[:, 0], in0=acc_rr[:], in1=t[:], op=ALU.add)
+            st["y", g] = y
+
+        def relu(g):
+            if g < 0 or g >= N:
+                return
+            n = GROUPS[g]
+            c, off = chunk_of(RES_CHUNKS, first[g])
+            m = RES_CHUNKS[c]
+            if off == 0:
+                st["res", c] = epi.tile([P, 2, m, F], F32, name="res", tag="res")
+            res = st["res", c]
+            nc.scalar.activation(out=res[:, :, off : off + n, :], in_=st["y", g][:], func=ACT.Relu)
+            if off + n == m:
+                nc.sync.dma_start(out=o0[:, :, first[g] + n - m : first[g] + n, :], in_=res[:])
+
+        def row_max(g):
+            if g < 0 or g >= N:
+                return
+            n = GROUPS[g]
+            amax = sml.tile([P, 2 * n], F32, name="amax", tag="amax")
+            nc.vector.tensor_reduce(out=amax[:], in_=st["y", g][:].rearrange("p r q f -> p (r q) f"), axis=AX.X, op=ALU.max)
+            st["amax", g] = amax
+
+        def row_rcp(g):
+            if g < 0 or g >= N:
+                return
+            n = GROUPS[g]
+            rcp = sml.tile([P, 2 * n], F32, name="rcp", tag="rcp")
+            nc.vector.reciprocal(out=rcp[:], in_=st["amax", g][:])
+            st["rcp", g] = rcp
+
+        def row_fac(g):
+            if g < 0 or g >= N:
+                return
+            n = GROUPS[g]
+            fac = sml.tile([P, 2 * n], F32, name="fac", tag="fac")
+            nc.scalar.activation(out=fac[:], in_=st["rcp", g][:], func=ACT.Copy, scale=448.0)
+            st["fac", g] = fac
+
+        def casts(g):
+            if g < 0 or g >= N:
+                return
+            n = GROUPS[g]
+            fac = st["fac", g]
+            c, off = chunk_of(RES_CHUNKS, first[g])
+            res = st["res", c]
+            cb, offb = chunk_of(BYTE_CHUNKS, first[g])
+            mb = BYTE_CHUNKS[cb]
+            if offb == 0:
+                st["byt", cb] = const.tile([P, 2, mb, F], FP8, name="byt%d" % cb)
+            byt = st["byt", cb]
+            for s in range(2 * n):
+                r, q = s // n, s % n
+                if s < V_CASTS[g]:
+                    nc.vector.tensor_scalar(
+                        out=byt[:, r, offb + q, :], in0=res[:, r, off + q, :], scalar1=fac[:, s : s + 1], scalar2=None, op0=ALU.mult, saturate=False
+                    )
+                else:
+                    nc.scalar.activation(
+                        out=byt[:, r, offb + q, :], in_=res[:, r, off + q, :], func=ACT.Identity, scale=fac[:, s : s + 1], bias=zero[:, 0:1], saturate=False
+                    )
+            if offb + n == mb:
+                for r in range(2):
+                    nc.sync.dma_start(out=o1[:, r, first[g] + n - mb : first[g] + n, :], in_=byt[:, r].bitcast(U8))
+
+        def bias_product():
+            bp = pt.tile([P, 2, F], F32, name="bp", tag="xt")
+            nc.tensor.matmul(out=bp[:].rearrange("p r f -> p (r f)"), lhsT=ones[:], rhs=brow[:], start=True, stop=True)
+            st["bp", 0] = bp
+
+        brow = const.tile([P, 2 * F], BF16, name="brow")
+        nc.gpsimd.memset(brow[:], 0.0)
+        nc.sync.dma_start(out=brow[0:1, 0:F], in_=b_r.rearrange("(o f) -> o f", o=1))
+        nc.sync.dma_start(out=brow[0:1, F : 2 * F], in_=b_i.rearrange("(o f) -> o f", o=1))
+        for g in range(LOADS_AHEAD):
+            load(g)
+        zero = const.tile([P, 1], F32, name="zero")
+        nc.vector.memset(zero[:], 0.0)
+        warm = const.tile([P, 1], F32, name="warm")
+        nc.scalar.activation(out=warm[:], in_=zero[:], func=ACT.Relu)
+        ident = const.tile([P, P], F32, name="ident")
+        make_identity(nc, ident[:])
+        ones = const.tile([P, P], BF16, name="ones")
+        nc.vector.memset(ones[:], 1.0)
+        bias = const.tile([P, 2, F], F32, name="bias")
+
+        for i in range(-2, N + 2):
+            if ORDER == "F":
+                quant_w(i)
+                products(i)
+                transposes(i + 2)
+                if i == -2:
+                    bias_product()
+                x_alloc(i + 1)
+                x_copies(i + 1, "s")
+                row_max(i - 1)
+                relu(i - 1)
+                w_alloc(i + 1)
+                w_interleave(i + 1, "v0")
+                row_rcp(i - 1)
+                w_interleave(i + 1, "v1")
+                row_fac(i - 1)
+                w_interleave(i + 1, "s")
+                quant_x(i + 1)
+                casts(i - 1)
+                if i == 0:
+                    nc.vector.tensor_copy(out=bias[:], in_=st["bp", 0][:])
+                sums(i)
+            else:
+                quant_x(i)
+                quant_w(i)
+                products(i)
+                transposes(i + 2)
+                if i == -2:
+                    bias_product()
+                x_alloc(i + 1)
+                x_copies(i + 1, "s")
+                w_alloc(i + 1)
+                w_interleave(i + 1, "g")
+                w_interleave(i + 1, "v0")
+                w_interleave(i + 1, "v1")
+                row_max(i - 1)
+                relu(i - 1)
+                row_rcp(i - 1)
+                row_fac(i - 1)
+                x_copies(i + 1, "v")
+                w_interleave(i + 1, "s")
+                casts(i - 1)
+                if i == 0:
+                    nc.vector.tensor_copy(out=bias[:], in_=st["bp", 0][:])
+                sums(i)
+            load(i + 2 + LOADS_AHEAD)

@@ -15,21 +15,26 @@ AX = mybir.AxisListType
 
 P = 128
 B, PIX, C, F = 128, 32, 512, 128
-GMAX = 4
+FLT_MAX = 3.4028234663852886e38
 
 FLOPS = 4 * PIX * 2 * B * C * F
 
-GROUPS = [2,2,2,2,4,4,4,4,4,2,2]
-X_CHUNKS = [2,2,2,2,4,4,4,4,4,2,2]
-RES_CHUNKS = [8,8,8,4,2,2]
-BYTE_CHUNKS = [16,8,4,2,2]
-V_SLICES = [2,0,0,0,0,0,0,0,0,0,0]
-G_SLICES = [0,2,2,2,4,4,4,4,4,2,2]
-V_BANKS = [0,0,0,0,1,1,1,1,1,0,0]
-V_CASTS = [0,0,0,0,0,0,0,0,0,0,2]
-LOADS_AHEAD = 3
-BLOCKED = "vs"
-ORDER = "H"
+GROUPS = [2, 2, 4, 4, 4, 4, 4, 4, 2, 2]
+RES_CHUNKS = [8, 8, 8, 4, 2, 2]
+BYTE_CHUNKS = [16, 8, 4, 2, 2]
+W_PLAN = {0: "vvss", 2: "ggss", 4: "ggggsspp"}
+V_BANKS = {2: 0, 4: 0}
+RELU_PLAN = {2: "gs", 4: "gs"}
+TAIL_RELU = "ss"
+TAIL_GROUPS = 2
+TAIL_V_CASTS = 1
+XT_BUFS = 4
+RES_BUFS = 3
+SPLIT_X_LOADS = 1
+BIAS_LOAD_AFTER = 1
+LOADS_FIRST = 3
+ORDER = [("quant_x", 0), ("quant_w", 0), ("products", 0), ("w_p_mm", 1), ("transposes", 2), ("w_g", 1), ("relu_g", -1), ("w_v", 1), ("row_max", -1), ("row_rcp", -1), ("x_v", 1), ("relu_s", -1), ("store_res", -1), ("x_s", 1), ("w_s", 1), ("row_fac", -1), ("w_p_copy", 1), ("casts_soon", -1), ("casts_late", -2), ("sums", 0), ("load", 5)]
+BIAS_AT = -1
 
 
 def starts(sizes):
@@ -43,6 +48,17 @@ def chunk_of(sizes, pixel):
     raise ValueError("pixel out of range")
 
 
+def runs(plan, letter):
+    out = []
+    for s in range(len(plan)):
+        if plan[s] == letter:
+            if out and out[-1][1] == s:
+                out[-1][1] = s + 1
+            else:
+                out.append([s, s + 1])
+    return out
+
+
 def tile_dot_pa_kernel(tc, x_crop, W_r, W_i, b_r, b_i, out_0, out_1):
     nc = tc.nc
     x = x_crop.rearrange("b r h w c -> b r (h w) c")
@@ -54,7 +70,7 @@ def tile_dot_pa_kernel(tc, x_crop, W_r, W_i, b_r, b_i, out_0, out_1):
     o1 = out_1.rearrange("b r h w f -> b r (h w) f")
     N = len(GROUPS)
     first = starts(GROUPS)
-    assert sum(GROUPS) == PIX and sum(X_CHUNKS) == PIX and sum(RES_CHUNKS) == PIX and sum(BYTE_CHUNKS) == PIX
+    assert sum(GROUPS) == PIX and sum(RES_CHUNKS) == PIX and sum(BYTE_CHUNKS) == PIX
 
     with ExitStack() as ctx:
         const = ctx.enter_context(tc.tile_pool(name="const", bufs=1))
@@ -63,99 +79,93 @@ def tile_dot_pa_kernel(tc, x_crop, W_r, W_i, b_r, b_i, out_0, out_1):
         code = ctx.enter_context(tc.tile_pool(name="code", bufs=2))
         epi = ctx.enter_context(tc.tile_pool(name="epi", bufs=2))
         sml = ctx.enter_context(tc.tile_pool(name="sml", bufs=3))
-        pt = ctx.enter_context(tc.psum_pool(name="pt", bufs=5))
+        pt = ctx.enter_context(tc.psum_pool(name="pt", bufs=XT_BUFS))
         pa = ctx.enter_context(tc.psum_pool(name="pa", bufs=1))
         ctx.enter_context(tc.manual_schedule())
 
         st = {}
 
-        def pixels(g):
-            return slice(first[g], first[g] + GROUPS[g])
+        def w_plan(g):
+            return W_PLAN[0] if g == 0 else W_PLAN[GROUPS[g]]
+
+        def relu_plan(g):
+            return TAIL_RELU if g >= N - TAIL_GROUPS else RELU_PLAN[GROUPS[g]]
 
         def load(g):
-            if g < 0 or g >= N:
-                return
             n = GROUPS[g]
-            c, off = chunk_of(X_CHUNKS, first[g])
-            if off == 0:
-                m = X_CHUNKS[c]
-                xr = raw.tile([P, 2, m, C], BF16, name="x_raw%d" % c)
-                nc.sync.dma_start(out=xr[:], in_=x[:, :, first[g] : first[g] + m, :])
-                st["x_raw", c] = xr
+            px = slice(first[g], first[g] + n)
+            xr = raw.tile([P, 2, n, C], BF16, name="x_raw%d" % g)
+            if g < SPLIT_X_LOADS:
+                for q in range(n):
+                    nc.sync.dma_start(out=xr[:, :, q, :], in_=x[:, :, first[g] + q, :])
+            else:
+                nc.sync.dma_start(out=xr[:], in_=x[:, :, px, :])
+            st["x_raw", g] = xr
             wr = raw.tile([P, 2, n, 4, F], BF16, name="w_raw%d" % g)
-            nc.sync.dma_start(out=wr[:, 0], in_=w_dram[0][:, pixels(g)])
-            nc.sync.dma_start(out=wr[:, 1], in_=w_dram[1][:, pixels(g)])
+            nc.sync.dma_start(out=wr[:, 0], in_=w_dram[0][:, px])
+            nc.sync.dma_start(out=wr[:, 1], in_=w_dram[1][:, px])
             st["w_raw", g] = wr
 
         def transposes(g):
-            if g < 0 or g >= N:
-                return
             n = GROUPS[g]
-            c, off = chunk_of(X_CHUNKS, first[g])
-            m = X_CHUNKS[c]
-            words = st["x_raw", c][:].rearrange("b r q c -> b (r q c)").bitcast(F32)
+            words = st["x_raw", g][:].rearrange("b r q c -> b (r q c)").bitcast(F32)
             banks = []
             for h in range(n):
                 xt = pt.tile([P, 2, 2, B], F32, name="xt", tag="xt")
-                for i in range(2):
-                    s = 2 * h + i
-                    row = (s // n) * m + off + s % n
+                for r in range(2):
+                    s = r * n + h
                     for u in range(2):
-                        nc.tensor.transpose(xt[:, i, u, :], words[:, 256 * row + u : 256 * (row + 1) : 2], ident[:])
+                        nc.tensor.transpose(xt[:, r, u, :], words[:, 256 * s + u : 256 * (s + 1) : 2], ident[:])
                 banks.append(xt)
             st["xt", g] = banks
 
-        def x_alloc(g):
-            if g < 0 or g >= N:
-                return
-            st["xg", g] = grp.tile([P, 2 * GROUPS[g], B, 4], BF16, name="xg", tag="xg", align_bytes=64)
-
         def x_copies(g, eng):
-            if g < 0 or g >= N:
-                return
             n = GROUPS[g]
+            if ("xg", g) not in st:
+                st["xg", g] = grp.tile([P, 2 * n, B, 4], BF16, name="xg", tag="xg", align_bytes=64)
             xg_w = st["xg", g][:].rearrange("p s b t -> p (s b t)").bitcast(F32).rearrange("p (s b u) -> p s b u", s=2 * n, u=2)
             for h in range(n):
                 src = st["xt", g][h][:].rearrange("p i u b -> p i b u")
-                on_v = h >= n - V_BANKS[g]
+                on_v = h >= n - V_BANKS[n]
                 if on_v and eng == "v":
                     nc.vector.tensor_copy(out=xg_w[:, 2 * h : 2 * h + 2], in_=src)
                 if not on_v and eng == "s":
                     nc.scalar.copy(out=xg_w[:, 2 * h : 2 * h + 2], in_=src)
 
-        def w_alloc(g):
-            if g < 0 or g >= N:
-                return
-            st["wg", g] = grp.tile([P, 2 * GROUPS[g], F, 4], BF16, name="wg", tag="wg", align_bytes=64, bufs=1)
+        def wg_of(g):
+            if ("wg", g) not in st:
+                st["wg", g] = grp.tile([P, 2 * GROUPS[g], F, 4], BF16, name="wg", tag="wg", align_bytes=64, bufs=1)
+            return st["wg", g]
 
-        def w_interleave(g, part):
-            if g < 0 or g >= N:
-                return
-            n = GROUPS[g]
-            a = V_SLICES[g]
-            e = a + G_SLICES[g]
-            h = a // 2 if a >= 4 else a
-            lo, hi = {"v0": (0, h), "v1": (h, a), "g": (a, e), "s": (e, 2 * n)}[part]
-            if hi <= lo:
-                return
-            wg = st["wg", g]
-            w_src = st["w_raw", g][:].rearrange("p w q j f -> p (w q) f j")
-            blk_dst = wg[:, lo:hi].rearrange("p s (c i) j -> p s c j i", i=4)
-            blk_src = st["w_raw", g][:].rearrange("p w q j f -> p (w q) j f")[:, lo:hi].rearrange("p s j (c i) -> p s c j i", i=4)
-            if part == "s" and "s" in BLOCKED:
-                nc.scalar.copy(out=blk_dst, in_=blk_src)
-            elif part in ("v0", "v1") and "v" in BLOCKED:
-                nc.vector.tensor_copy(out=blk_dst, in_=blk_src)
-            elif part == "s":
-                nc.scalar.copy(out=wg[:, lo:hi], in_=w_src[:, lo:hi])
-            elif part == "g":
-                nc.gpsimd.tensor_scalar(out=wg[:, lo:hi], in0=w_src[:, lo:hi], scalar1=1.0, scalar2=0.0, op0=ALU.mult, op1=ALU.add)
-            else:
-                nc.vector.tensor_copy(out=wg[:, lo:hi], in_=w_src[:, lo:hi])
+        def w_copies(g, letter):
+            for lo, hi in runs(w_plan(g), letter):
+                wg = wg_of(g)
+                slots = st["w_raw", g][:].rearrange("p w q j f -> p (w q) j f")
+                blk_dst = wg[:, lo:hi].rearrange("p s (c i) j -> p s c j i", i=4)
+                blk_src = slots[:, lo:hi].rearrange("p s j (c i) -> p s c j i", i=4)
+                if letter == "s":
+                    nc.scalar.copy(out=blk_dst, in_=blk_src)
+                elif letter == "v":
+                    nc.vector.tensor_copy(out=blk_dst, in_=blk_src)
+                else:
+                    nc.gpsimd.tensor_scalar(
+                        out=wg[:, lo:hi], in0=slots[:, lo:hi].rearrange("p s j f -> p s f j"), scalar1=1.0, scalar2=0.0, op0=ALU.mult, op1=ALU.add
+                    )
+
+        def w_p_mm(g):
+            slots = st["w_raw", g][:].rearrange("p w q j f -> p (w q) j f")
+            for lo, hi in runs(w_plan(g), "p"):
+                assert hi - lo == 2
+                wp = pt.tile([P, 2, F, 4], BF16, name="wp", tag="wp", bufs=1)
+                for h in range(2):
+                    nc.tensor.matmul(out=wp[:, h], lhsT=ident_bf[:], rhs=slots[:, lo + h].rearrange("p j f -> p f j"), start=True, stop=True)
+                st["wp", g, lo] = wp
+
+        def w_p_copy(g):
+            for lo, hi in runs(w_plan(g), "p"):
+                nc.scalar.copy(out=wg_of(g)[:, lo:hi], in_=st["wp", g, lo][:])
 
         def quant_x(g):
-            if g < 0 or g >= N:
-                return
             n = GROUPS[g]
             xc = code.tile([P, 2 * n * B], U32, name="xc", tag="xc", align_bytes=64)
             xs = code.tile([P, 2 * n * B], U8, name="xs", tag="xs", align_bytes=64)
@@ -163,8 +173,6 @@ def tile_dot_pa_kernel(tc, x_crop, W_r, W_i, b_r, b_i, out_0, out_1):
             st["qx", g] = (xc, xs)
 
         def quant_w(g):
-            if g < 0 or g >= N:
-                return
             n = GROUPS[g]
             wc = code.tile([P, 2 * n * F], U32, name="wc", tag="wc", align_bytes=64)
             ws = code.tile([P, 2 * n * F], U8, name="ws", tag="ws", align_bytes=64)
@@ -172,14 +180,19 @@ def tile_dot_pa_kernel(tc, x_crop, W_r, W_i, b_r, b_i, out_0, out_1):
             st["qw", g] = (wc, ws)
 
         def products(g):
-            if g < 0 or g >= N:
-                return
             n = GROUPS[g]
             xc, xs = st["qx", g]
             wc, ws = st["qw", g]
             acc_rr = pa.tile([P, n, F], F32, name="acc_rr", tag="acc_rr")
-            acc_ii = pa.tile([P, n, F], F32, name="acc_ii", tag="acc_ii")
-            acc_im = pa.tile([P, n, F], F32, name="acc_im", tag="acc_im")
+            if n <= 2:
+                both = pa.tile([P, 2, n, F], F32, name="acc_both", tag="acc_im")
+                acc_im, acc_ii = both[:, 0], both[:, 1]
+                st["acc", g] = (acc_rr, both)
+            else:
+                im = pa.tile([P, n, F], F32, name="acc_im", tag="acc_im")
+                ii = pa.tile([P, n, F], F32, name="acc_ii", tag="acc_ii")
+                acc_im, acc_ii = im[:], ii[:]
+                st["acc", g] = (acc_rr, im, ii)
 
             def mm(out, sx, sw, start, stop):
                 cx = slice(B * sx, B * (sx + 1))
@@ -195,85 +208,85 @@ def tile_dot_pa_kernel(tc, x_crop, W_r, W_i, b_r, b_i, out_0, out_1):
                 )
 
             for q in range(n):
-                mm(acc_ii[:, q, :], n + q, n + q, True, True)
+                mm(acc_ii[:, q, :], 2 * q + 1, n + q, True, True)
             for q in range(n):
-                mm(acc_im[:, q, :], n + q, q, True, False)
-                mm(acc_im[:, q, :], q, n + q, False, True)
+                mm(acc_im[:, q, :], 2 * q + 1, q, True, False)
+                mm(acc_im[:, q, :], 2 * q, n + q, False, True)
             for q in range(n):
-                mm(acc_rr[:, q, :], q, q, True, True)
-            st["acc", g] = (acc_rr, acc_ii, acc_im)
+                mm(acc_rr[:, q, :], 2 * q, q, True, True)
 
         def sums(g):
-            if g < 0 or g >= N:
-                return
             n = GROUPS[g]
-            acc_rr, acc_ii, acc_im = st["acc", g]
-            t = epi.tile([P, n, F], F32, name="t", tag="t")
-            y = epi.tile([P, 2, n, F], F32, name="y", tag="y")
-            nc.vector.scalar_tensor_tensor(
-                out=t[:],
-                in0=acc_ii[:],
-                scalar=-1.0,
-                in1=bias[:, 0:1, :].to_broadcast([P, n, F]),
-                op0=ALU.mult,
-                op1=ALU.add,
-            )
-            nc.vector.tensor_tensor(out=y[:, 1], in0=acc_im[:], in1=bias[:, 1:2, :].to_broadcast([P, n, F]), op=ALU.add)
-            nc.vector.tensor_tensor(out=y[:, 0], in0=acc_rr[:], in1=t[:], op=ALU.add)
+            y = epi.tile([P, 3, n, F], F32, name="y", tag="y")
+            acc = st["acc", g]
+            if n <= 2:
+                nc.vector.tensor_tensor(
+                    out=y[:, 1:3], in0=acc[1][:], in1=bias[:].rearrange("p (k o) f -> p k o f", o=1).to_broadcast([P, 2, n, F]), op=ALU.add
+                )
+            else:
+                nc.vector.tensor_tensor(out=y[:, 2], in0=acc[2][:], in1=bias[:, 1:2, :].to_broadcast([P, n, F]), op=ALU.add)
+                nc.vector.tensor_tensor(out=y[:, 1], in0=acc[1][:], in1=bias[:, 0:1, :].to_broadcast([P, n, F]), op=ALU.add)
+            nc.vector.tensor_tensor(out=y[:, 0], in0=acc[0][:], in1=y[:, 2], op=ALU.subtract)
             st["y", g] = y
 
-        def relu(g):
-            if g < 0 or g >= N:
+        def res_of(g):
+            c, off = chunk_of(RES_CHUNKS, first[g])
+            if ("res", c) not in st:
+                st["res", c] = epi.tile([P, 2, RES_CHUNKS[c], F], F32, name="res", tag="res", bufs=RES_BUFS)
+            return st["res", c], off
+
+        def relu(g, eng):
+            n = GROUPS[g]
+            plan = relu_plan(g)
+            parts = [r for r in range(2) if plan[r] == eng]
+            if not parts:
                 return
+            res, off = res_of(g)
+            lo, hi = parts[0], parts[-1] + 1
+            dst = res[:, lo:hi, off : off + n, :]
+            src = st["y", g][:, lo:hi]
+            if eng == "s":
+                nc.scalar.activation(out=dst, in_=src, func=ACT.Relu)
+            elif eng == "v":
+                nc.vector.tensor_scalar(out=dst, in0=src, scalar1=0.0, scalar2=None, op0=ALU.max)
+            else:
+                nc.gpsimd.tensor_scalar(out=dst, in0=src, scalar1=FLT_MAX, scalar2=0.0, op0=ALU.min, op1=ALU.max)
+
+        def store_res(g):
             n = GROUPS[g]
             c, off = chunk_of(RES_CHUNKS, first[g])
             m = RES_CHUNKS[c]
-            if off == 0:
-                st["res", c] = epi.tile([P, 2, m, F], F32, name="res", tag="res")
-            res = st["res", c]
-            nc.scalar.activation(out=res[:, :, off : off + n, :], in_=st["y", g][:], func=ACT.Relu)
             if off + n == m:
-                nc.sync.dma_start(out=o0[:, :, first[g] + n - m : first[g] + n, :], in_=res[:])
+                nc.sync.dma_start(out=o0[:, :, first[g] + n - m : first[g] + n, :], in_=st["res", c][:])
 
         def row_max(g):
-            if g < 0 or g >= N:
-                return
             n = GROUPS[g]
             amax = sml.tile([P, 2 * n], F32, name="amax", tag="amax")
-            nc.vector.tensor_reduce(out=amax[:], in_=st["y", g][:].rearrange("p r q f -> p (r q) f"), axis=AX.X, op=ALU.max)
+            nc.vector.tensor_reduce(out=amax[:], in_=st["y", g][:, 0:2].rearrange("p r q f -> p (r q) f"), axis=AX.X, op=ALU.max)
             st["amax", g] = amax
 
         def row_rcp(g):
-            if g < 0 or g >= N:
-                return
-            n = GROUPS[g]
-            rcp = sml.tile([P, 2 * n], F32, name="rcp", tag="rcp")
+            rcp = sml.tile([P, 2 * GROUPS[g]], F32, name="rcp", tag="rcp")
             nc.vector.reciprocal(out=rcp[:], in_=st["amax", g][:])
             st["rcp", g] = rcp
 
         def row_fac(g):
-            if g < 0 or g >= N:
-                return
-            n = GROUPS[g]
-            fac = sml.tile([P, 2 * n], F32, name="fac", tag="fac")
+            fac = sml.tile([P, 2 * GROUPS[g]], F32, name="fac", tag="fac")
             nc.scalar.activation(out=fac[:], in_=st["rcp", g][:], func=ACT.Copy, scale=448.0)
             st["fac", g] = fac
 
-        def casts(g):
-            if g < 0 or g >= N:
-                return
+        def casts(g, r):
             n = GROUPS[g]
             fac = st["fac", g]
-            c, off = chunk_of(RES_CHUNKS, first[g])
-            res = st["res", c]
+            res, off = res_of(g)
             cb, offb = chunk_of(BYTE_CHUNKS, first[g])
             mb = BYTE_CHUNKS[cb]
-            if offb == 0:
+            if ("byt", cb) not in st:
                 st["byt", cb] = const.tile([P, 2, mb, F], FP8, name="byt%d" % cb)
             byt = st["byt", cb]
-            for s in range(2 * n):
-                r, q = s // n, s % n
-                if s < V_CASTS[g]:
+            for q in range(n):
+                s = r * n + q
+                if g == N - 1 and q < TAIL_V_CASTS:
                     nc.vector.tensor_scalar(
                         out=byt[:, r, offb + q, :], in0=res[:, r, off + q, :], scalar1=fac[:, s : s + 1], scalar2=None, op0=ALU.mult, saturate=False
                     )
@@ -282,20 +295,41 @@ def tile_dot_pa_kernel(tc, x_crop, W_r, W_i, b_r, b_i, out_0, out_1):
                         out=byt[:, r, offb + q, :], in_=res[:, r, off + q, :], func=ACT.Identity, scale=fac[:, s : s + 1], bias=zero[:, 0:1], saturate=False
                     )
             if offb + n == mb:
-                for r in range(2):
-                    nc.sync.dma_start(out=o1[:, r, first[g] + n - mb : first[g] + n, :], in_=byt[:, r].bitcast(U8))
+                nc.sync.dma_start(out=o1[:, r, first[g] + n - mb : first[g] + n, :], in_=byt[:, r].bitcast(U8))
 
-        def bias_product():
-            bp = pt.tile([P, 2, F], F32, name="bp", tag="xt")
-            nc.tensor.matmul(out=bp[:].rearrange("p r f -> p (r f)"), lhsT=ones[:], rhs=brow[:], start=True, stop=True)
-            st["bp", 0] = bp
+        stages = {
+            "load": load,
+            "transposes": transposes,
+            "x_s": lambda g: x_copies(g, "s"),
+            "x_v": lambda g: x_copies(g, "v"),
+            "w_g": lambda g: w_copies(g, "g"),
+            "w_s": lambda g: w_copies(g, "s"),
+            "w_v": lambda g: w_copies(g, "v"),
+            "w_p_mm": w_p_mm,
+            "w_p_copy": w_p_copy,
+            "quant_x": quant_x,
+            "quant_w": quant_w,
+            "products": products,
+            "sums": sums,
+            "row_max": row_max,
+            "row_rcp": row_rcp,
+            "row_fac": row_fac,
+            "relu_s": lambda g: relu(g, "s"),
+            "relu_v": lambda g: relu(g, "v"),
+            "relu_g": lambda g: relu(g, "g"),
+            "store_res": store_res,
+            "casts_soon": lambda g: [casts(g, r) for r in (1, 0) if relu_plan(g)[r] != "g"],
+            "casts_late": lambda g: [casts(g, r) for r in (1, 0) if relu_plan(g)[r] == "g"],
+        }
 
         brow = const.tile([P, 2 * F], BF16, name="brow")
         nc.gpsimd.memset(brow[:], 0.0)
-        nc.sync.dma_start(out=brow[0:1, 0:F], in_=b_r.rearrange("(o f) -> o f", o=1))
-        nc.sync.dma_start(out=brow[0:1, F : 2 * F], in_=b_i.rearrange("(o f) -> o f", o=1))
-        for g in range(LOADS_AHEAD):
-            load(g)
+        for g in range(LOADS_FIRST + 1):
+            if g == BIAS_LOAD_AFTER:
+                nc.sync.dma_start(out=brow[0:1, 0:F], in_=b_i.rearrange("(o f) -> o f", o=1))
+                nc.sync.dma_start(out=brow[0:1, F : 2 * F], in_=b_r.rearrange("(o f) -> o f", o=1))
+            if g < LOADS_FIRST:
+                load(g)
         zero = const.tile([P, 1], F32, name="zero")
         nc.vector.memset(zero[:], 0.0)
         warm = const.tile([P, 1], F32, name="warm")
@@ -305,50 +339,22 @@ def tile_dot_pa_kernel(tc, x_crop, W_r, W_i, b_r, b_i, out_0, out_1):
         ones = const.tile([P, P], BF16, name="ones")
         nc.vector.memset(ones[:], 1.0)
         bias = const.tile([P, 2, F], F32, name="bias")
+        if any("p" in plan for plan in W_PLAN.values()):
+            ident_bf = const.tile([P, P], BF16, name="ident_bf")
+            make_identity(nc, ident_bf[:])
 
-        for i in range(-2, N + 2):
-            if ORDER == "F":
-                quant_w(i)
-                products(i)
-                transposes(i + 2)
-                if i == -2:
-                    bias_product()
-                x_alloc(i + 1)
-                x_copies(i + 1, "s")
-                row_max(i - 1)
-                relu(i - 1)
-                w_alloc(i + 1)
-                w_interleave(i + 1, "v0")
-                row_rcp(i - 1)
-                w_interleave(i + 1, "v1")
-                row_fac(i - 1)
-                w_interleave(i + 1, "s")
-                quant_x(i + 1)
-                casts(i - 1)
-                if i == 0:
-                    nc.vector.tensor_copy(out=bias[:], in_=st["bp", 0][:])
-                sums(i)
-            else:
-                quant_x(i)
-                quant_w(i)
-                products(i)
-                transposes(i + 2)
-                if i == -2:
-                    bias_product()
-                x_alloc(i + 1)
-                x_copies(i + 1, "s")
-                w_alloc(i + 1)
-                w_interleave(i + 1, "g")
-                w_interleave(i + 1, "v0")
-                w_interleave(i + 1, "v1")
-                row_max(i - 1)
-                relu(i - 1)
-                row_rcp(i - 1)
-                row_fac(i - 1)
-                x_copies(i + 1, "v")
-                w_interleave(i + 1, "s")
-                casts(i - 1)
-                if i == 0:
-                    nc.vector.tensor_copy(out=bias[:], in_=st["bp", 0][:])
-                sums(i)
-            load(i + 2 + LOADS_AHEAD)
+        lags = [lag for name, lag in ORDER]
+        for i in range(-max(lags), N - min(lags)):
+            for name, lag in ORDER:
+                g = i + lag
+                if name == "load" and g < LOADS_FIRST:
+                    continue
+                if name == "sums" and g == 0:
+                    nc.vector.tensor_copy(out=bias[:, 0], in_=st["bp", 0][:, 0])
+                    nc.vector.tensor_scalar(out=bias[:, 1], in0=st["bp", 0][:, 1], scalar1=-1.0, scalar2=None, op0=ALU.mult)
+                if 0 <= g < N:
+                    stages[name](g)
+                if name == "transposes" and i == BIAS_AT:
+                    bp = pt.tile([P, 2, F], F32, name="bp", tag="xt")
+                    nc.tensor.matmul(out=bp[:].rearrange("p r f -> p (r f)"), lhsT=ones[:], rhs=brow[:], start=True, stop=True)
+                    st["bp", 0] = bp

@@ -19,21 +19,21 @@ FLT_MAX = 3.4028234663852886e38
 
 FLOPS = 4 * PIX * 2 * B * C * F
 
-GROUPS = [2, 2, 4, 4, 4, 4, 4, 4, 2, 2]
+GROUPS = [2, 2, 2, 2, 4, 4, 4, 4, 4, 2, 2]
 RES_CHUNKS = [8, 8, 8, 4, 2, 2]
 BYTE_CHUNKS = [16, 8, 4, 2, 2]
-W_PLAN = {0: "vvss", 2: "ggss", 4: "ggggsspp"}
-V_BANKS = {2: 0, 4: 0}
-RELU_PLAN = {2: "gs", 4: "gs"}
+W_PLAN = {0: "vvss", 2: "ggss", 4: "ggggssss"}
+V_BANKS = {2: 0, 4: 1}
+RELU_PLAN = {2: "ss", 4: "ss"}
 TAIL_RELU = "ss"
-TAIL_GROUPS = 2
+TAIL_GROUPS = 1
 TAIL_V_CASTS = 1
-XT_BUFS = 4
+XT_BUFS = 5
 RES_BUFS = 3
 SPLIT_X_LOADS = 1
 BIAS_LOAD_AFTER = 1
 LOADS_FIRST = 3
-ORDER = [("quant_x", 0), ("quant_w", 0), ("products", 0), ("w_p_mm", 1), ("transposes", 2), ("w_g", 1), ("relu_g", -1), ("w_v", 1), ("row_max", -1), ("row_rcp", -1), ("x_v", 1), ("relu_s", -1), ("store_res", -1), ("x_s", 1), ("w_s", 1), ("row_fac", -1), ("w_p_copy", 1), ("casts_soon", -1), ("casts_late", -2), ("sums", 0), ("load", 5)]
+ORDER = [("quant_x", 0), ("quant_w", 0), ("products", 0), ("w_p_mm", 1), ("transposes", 2), ("x_s", 1), ("w_g", 1), ("relu_g", -1), ("w_v", 1), ("row_max", -1), ("relu_s", -1), ("relu_v", -1), ("store_res", -1), ("row_rcp", -1), ("row_fac", -1), ("x_v", 1), ("w_s", 1), ("w_p_copy", 1), ("casts_soon", -1), ("casts_late", -2), ("sums", 0), ("load", 5)]
 BIAS_AT = -1
 
 

@@ -22,19 +22,20 @@ FLOPS = 4 * PIX * 2 * B * C * F
 GROUPS = [2, 2, 2, 2, 4, 4, 4, 4, 4, 2, 2]
 RES_CHUNKS = [8, 8, 8, 4, 2, 2]
 BYTE_CHUNKS = [16, 8, 4, 2, 2]
-W_PLAN = {0: "vvss", 2: "ggss", 4: "ggggssss"}
+W_PLAN = {0: "vvsg", 2: "ggss", 4: "ggggssss"}
 V_BANKS = {2: 0, 4: 1}
 RELU_PLAN = {2: "ss", 4: "ss"}
 TAIL_RELU = "ss"
 TAIL_GROUPS = 1
 TAIL_V_CASTS = 1
 XT_BUFS = 5
-RES_BUFS = 3
+MERGE_MAX = 0
+RES_BUFS = 2
 SPLIT_X_LOADS = 1
-BIAS_LOAD_AFTER = 1
+BIAS_LOAD_AFTER = -1
 LOADS_FIRST = 3
-ORDER = [("quant_x", 0), ("quant_w", 0), ("products", 0), ("w_p_mm", 1), ("transposes", 2), ("x_s", 1), ("w_g", 1), ("relu_g", -1), ("w_v", 1), ("row_max", -1), ("relu_s", -1), ("relu_v", -1), ("store_res", -1), ("row_rcp", -1), ("row_fac", -1), ("x_v", 1), ("w_s", 1), ("w_p_copy", 1), ("casts_soon", -1), ("casts_late", -2), ("sums", 0), ("load", 5)]
-BIAS_AT = -1
+ORDER = [("quant_x", 0), ("quant_w", 0), ("products", 0), ("w_p_mm", 1), ("transposes", 2), ("x_s", 1), ("w_g", 1), ("relu_g", -1), ("w_v", 1), ("row_max", -1), ("relu_s", -1), ("relu_v", -1), ("store_res", -1), ("row_rcp", -1), ("row_fac", -1), ("x_v", 1), ("w_s", 1), ("w_p_copy", 1), ("casts_soon", -1), ("casts_late", -2), ("sums_a", 0), ("sums_b", 0), ("load", 5)]
+BIAS_AT = -9
 
 
 def starts(sizes):
@@ -98,6 +99,8 @@ def tile_dot_pa_kernel(tc, x_crop, W_r, W_i, b_r, b_i, out_0, out_1):
             if g < SPLIT_X_LOADS:
                 for q in range(n):
                     nc.sync.dma_start(out=xr[:, :, q, :], in_=x[:, :, first[g] + q, :])
+                    if g == 0 and q == 0 and BIAS_LOAD_AFTER < 0:
+                        load_bias()
             else:
                 nc.sync.dma_start(out=xr[:], in_=x[:, :, px, :])
             st["x_raw", g] = xr
@@ -184,7 +187,7 @@ def tile_dot_pa_kernel(tc, x_crop, W_r, W_i, b_r, b_i, out_0, out_1):
             xc, xs = st["qx", g]
             wc, ws = st["qw", g]
             acc_rr = pa.tile([P, n, F], F32, name="acc_rr", tag="acc_rr")
-            if n <= 2:
+            if n <= MERGE_MAX:
                 both = pa.tile([P, 2, n, F], F32, name="acc_both", tag="acc_im")
                 acc_im, acc_ii = both[:, 0], both[:, 1]
                 st["acc", g] = (acc_rr, both)
@@ -215,19 +218,25 @@ def tile_dot_pa_kernel(tc, x_crop, W_r, W_i, b_r, b_i, out_0, out_1):
             for q in range(n):
                 mm(acc_rr[:, q, :], 2 * q, q, True, True)
 
-        def sums(g):
+        def sums_a(g):
             n = GROUPS[g]
             y = epi.tile([P, 3, n, F], F32, name="y", tag="y")
             acc = st["acc", g]
-            if n <= 2:
+            if n <= MERGE_MAX:
                 nc.vector.tensor_tensor(
                     out=y[:, 1:3], in0=acc[1][:], in1=bias[:].rearrange("p (k o) f -> p k o f", o=1).to_broadcast([P, 2, n, F]), op=ALU.add
                 )
             else:
                 nc.vector.tensor_tensor(out=y[:, 2], in0=acc[2][:], in1=bias[:, 1:2, :].to_broadcast([P, n, F]), op=ALU.add)
+            st["y", g] = y
+
+        def sums_b(g):
+            n = GROUPS[g]
+            y = st["y", g]
+            acc = st["acc", g]
+            if n > MERGE_MAX:
                 nc.vector.tensor_tensor(out=y[:, 1], in0=acc[1][:], in1=bias[:, 0:1, :].to_broadcast([P, n, F]), op=ALU.add)
             nc.vector.tensor_tensor(out=y[:, 0], in0=acc[0][:], in1=y[:, 2], op=ALU.subtract)
-            st["y", g] = y
 
         def res_of(g):
             c, off = chunk_of(RES_CHUNKS, first[g])
@@ -297,6 +306,16 @@ def tile_dot_pa_kernel(tc, x_crop, W_r, W_i, b_r, b_i, out_0, out_1):
             if offb + n == mb:
                 nc.sync.dma_start(out=o1[:, r, first[g] + n - mb : first[g] + n, :], in_=byt[:, r].bitcast(U8))
 
+        def load_bias():
+            nc.sync.dma_start(out=brow[0:1, 0:F], in_=b_i.rearrange("(o f) -> o f", o=1))
+            nc.sync.dma_start(out=brow[0:1, F : 2 * F], in_=b_r.rearrange("(o f) -> o f", o=1))
+
+        def spread_bias():
+            bp = pt.tile([P, 2, F], F32, name="bp", tag="xt")
+            nc.tensor.matmul(out=bp[:].rearrange("p r f -> p (r f)"), lhsT=ones[:], rhs=brow[:], start=True, stop=True)
+            nc.vector.tensor_copy(out=bias[:, 0], in_=bp[:, 0])
+            nc.vector.tensor_scalar(out=bias[:, 1], in0=bp[:, 1], scalar1=-1.0, scalar2=None, op0=ALU.mult)
+
         stages = {
             "load": load,
             "transposes": transposes,
@@ -310,7 +329,8 @@ def tile_dot_pa_kernel(tc, x_crop, W_r, W_i, b_r, b_i, out_0, out_1):
             "quant_x": quant_x,
             "quant_w": quant_w,
             "products": products,
-            "sums": sums,
+            "sums_a": sums_a,
+            "sums_b": sums_b,
             "row_max": row_max,
             "row_rcp": row_rcp,
             "row_fac": row_fac,
@@ -326,8 +346,7 @@ def tile_dot_pa_kernel(tc, x_crop, W_r, W_i, b_r, b_i, out_0, out_1):
         nc.gpsimd.memset(brow[:], 0.0)
         for g in range(LOADS_FIRST + 1):
             if g == BIAS_LOAD_AFTER:
-                nc.sync.dma_start(out=brow[0:1, 0:F], in_=b_i.rearrange("(o f) -> o f", o=1))
-                nc.sync.dma_start(out=brow[0:1, F : 2 * F], in_=b_r.rearrange("(o f) -> o f", o=1))
+                load_bias()
             if g < LOADS_FIRST:
                 load(g)
         zero = const.tile([P, 1], F32, name="zero")
@@ -343,13 +362,15 @@ def tile_dot_pa_kernel(tc, x_crop, W_r, W_i, b_r, b_i, out_0, out_1):
             ident_bf = const.tile([P, P], BF16, name="ident_bf")
             make_identity(nc, ident_bf[:])
 
+        if BIAS_AT <= -9:
+            spread_bias()
         lags = [lag for name, lag in ORDER]
         for i in range(-max(lags), N - min(lags)):
             for name, lag in ORDER:
                 g = i + lag
                 if name == "load" and g < LOADS_FIRST:
                     continue
-                if name == "sums" and g == 0:
+                if name == "sums_a" and g == 0 and BIAS_AT > -9:
                     nc.vector.tensor_copy(out=bias[:, 0], in_=st["bp", 0][:, 0])
                     nc.vector.tensor_scalar(out=bias[:, 1], in0=st["bp", 0][:, 1], scalar1=-1.0, scalar2=None, op0=ALU.mult)
                 if 0 <= g < N:

@@ -23,12 +23,14 @@ GROUPS = [2, 2, 2, 2, 4, 4, 4, 4, 4, 2, 2]
 RES_CHUNKS = [8, 8, 8, 4, 2, 2]
 BYTE_CHUNKS = [16, 8, 4, 2, 2]
 W_PLAN = {0: "vvsg", 2: "ggss", 4: "ggggssss"}
-V_BANKS = {2: 0, 4: 1}
+V_BANKS = [0, 0, 0, 0, 1, 1, 1, 1, 1, 0, 0]
 RELU_PLAN = {2: "ss", 4: "ss"}
 TAIL_RELU = "ss"
 TAIL_GROUPS = 1
 TAIL_V_CASTS = 1
 XT_BUFS = 5
+BLOCK = 8
+G_BLOCK = 0
 MERGE_MAX = 0
 RES_BUFS = 2
 SPLIT_X_LOADS = 1
@@ -129,7 +131,7 @@ def tile_dot_pa_kernel(tc, x_crop, W_r, W_i, b_r, b_i, out_0, out_1):
             xg_w = st["xg", g][:].rearrange("p s b t -> p (s b t)").bitcast(F32).rearrange("p (s b u) -> p s b u", s=2 * n, u=2)
             for h in range(n):
                 src = st["xt", g][h][:].rearrange("p i u b -> p i b u")
-                on_v = h >= n - V_BANKS[n]
+                on_v = h >= n - V_BANKS[g]
                 if on_v and eng == "v":
                     nc.vector.tensor_copy(out=xg_w[:, 2 * h : 2 * h + 2], in_=src)
                 if not on_v and eng == "s":
@@ -144,12 +146,15 @@ def tile_dot_pa_kernel(tc, x_crop, W_r, W_i, b_r, b_i, out_0, out_1):
             for lo, hi in runs(w_plan(g), letter):
                 wg = wg_of(g)
                 slots = st["w_raw", g][:].rearrange("p w q j f -> p (w q) j f")
-                blk_dst = wg[:, lo:hi].rearrange("p s (c i) j -> p s c j i", i=4)
-                blk_src = slots[:, lo:hi].rearrange("p s j (c i) -> p s c j i", i=4)
+                blk = G_BLOCK if letter == "g" else BLOCK
+                blk_dst = wg[:, lo:hi].rearrange("p s (c i) j -> p s c j i", i=max(blk, 1))
+                blk_src = slots[:, lo:hi].rearrange("p s j (c i) -> p s c j i", i=max(blk, 1))
                 if letter == "s":
                     nc.scalar.copy(out=blk_dst, in_=blk_src)
                 elif letter == "v":
                     nc.vector.tensor_copy(out=blk_dst, in_=blk_src)
+                elif blk > 0:
+                    nc.gpsimd.tensor_scalar(out=blk_dst, in0=blk_src, scalar1=1.0, scalar2=0.0, op0=ALU.mult, op1=ALU.add)
                 else:
                     nc.gpsimd.tensor_scalar(
                         out=wg[:, lo:hi], in0=slots[:, lo:hi].rearrange("p s j f -> p s f j"), scalar1=1.0, scalar2=0.0, op0=ALU.mult, op1=ALU.add

from contextlib import ExitStack

import concourse.mybir as mybir
from concourse.masks import make_identity

F32 = mybir.dt.float32
BF16 = mybir.dt.bfloat16
U32 = mybir.dt.uint32
U8 = mybir.dt.uint8
FP8X4 = mybir.dt.float8_e4m3fn_x4
FP8 = mybir.dt.float8_e4m3fn
ALU = mybir.AluOpType
ACT = mybir.ActivationFunctionType
AX = mybir.AxisListType

P = 128
B, PIX, C, F = 128, 32, 512, 128
FLT_MAX = 3.4028234663852886e38

FLOPS = 4 * PIX * 2 * B * C * F

GROUPS = [2, 2, 2, 2, 4, 4, 4, 4, 4, 2, 2]
RES_CHUNKS = [8, 8, 8, 4, 2, 2]
BYTE_CHUNKS = [16, 8, 4, 2, 2]
W_PLAN = {0: "vvsg", 2: "ggss", 4: "ggggssss"}
V_BANKS = [0, 0, 0, 0, 1, 1, 1, 1, 1, 0, 0]
RELU_PLAN = {2: "ss", 4: "ss"}
TAIL_RELU = "ss"
TAIL_GROUPS = 1
TAIL_V_CASTS = 1
XT_BUFS = 5
BLOCK = 8
G_BLOCK = 0
MERGE_MAX = 0
RES_BUFS = 2
SPLIT_X_LOADS = 1
BIAS_LOAD_AFTER = -1
LOADS_FIRST = 3
ORDER = [("quant_x", 0), ("quant_w", 0), ("products", 0), ("w_p_mm", 1), ("transposes", 2), ("x_s", 1), ("w_g", 1), ("relu_g", -1), ("w_v", 1), ("row_max", -1), ("relu_s", -1), ("relu_v", -1), ("store_res", -1), ("row_rcp", -1), ("row_fac", -1), ("x_v", 1), ("w_s", 1), ("w_p_copy", 1), ("casts_soon", -1), ("casts_late", -2), ("sums_a", 0), ("sums_b", 0), ("load", 5)]
BIAS_AT = -9


def starts(sizes):
    return [sum(sizes[:c]) for c in range(len(sizes))]


def chunk_of(sizes, pixel):
    for c, s in enumerate(starts(sizes)):
        if s <= pixel < s + sizes[c]:
            return c, pixel - s
    raise ValueError("pixel out of range")


def runs(plan, letter):
    out = []
    for s in range(len(plan)):
        if plan[s] == letter:
            if out and out[-1][1] == s:
                out[-1][1] = s + 1
            else:
                out.append([s, s + 1])
    return out


def tile_dot_pa_kernel(tc, x_crop, W_r, W_i, b_r, b_i, out_0, out_1):
    nc = tc.nc
    x = x_crop.rearrange("b r h w c -> b r (h w) c")
    w_dram = [
        W_r.rearrange("h w (p j) f -> p (h w) j f", j=4),
        W_i.rearrange("h w (p j) f -> p (h w) j f", j=4),
    ]
    o0 = out_0.rearrange("b r h w f -> b r (h w) f")
    o1 = out_1.rearrange("b r h w f -> b r (h w) f")
    N = len(GROUPS)
    first = starts(GROUPS)
    assert sum(GROUPS) == PIX and sum(RES_CHUNKS) == PIX and sum(BYTE_CHUNKS) == PIX

    with ExitStack() as ctx:
        const = ctx.enter_context(tc.tile_pool(name="const", bufs=1))
        raw = ctx.enter_context(tc.tile_pool(name="raw", bufs=1))
        grp = ctx.enter_context(tc.tile_pool(name="grp", bufs=2))
        code = ctx.enter_context(tc.tile_pool(name="code", bufs=2))
        epi = ctx.enter_context(tc.tile_pool(name="epi", bufs=2))
        sml = ctx.enter_context(tc.tile_pool(name="sml", bufs=3))
        pt = ctx.enter_context(tc.psum_pool(name="pt", bufs=XT_BUFS))
        pa = ctx.enter_context(tc.psum_pool(name="pa", bufs=1))
        ctx.enter_context(tc.manual_schedule())

        st = {}

        def w_plan(g):
            return W_PLAN[0] if g == 0 else W_PLAN[GROUPS[g]]

        def relu_plan(g):
            return TAIL_RELU if g >= N - TAIL_GROUPS else RELU_PLAN[GROUPS[g]]

        def load(g):
            n = GROUPS[g]
            px = slice(first[g], first[g] + n)
            xr = raw.tile([P, 2, n, C], BF16, name="x_raw%d" % g)
            if g < SPLIT_X_LOADS:
                for q in range(n):
                    nc.sync.dma_start(out=xr[:, :, q, :], in_=x[:, :, first[g] + q, :])
                    if g == 0 and q == 0 and BIAS_LOAD_AFTER < 0:
                        load_bias()
            else:
                nc.sync.dma_start(out=xr[:], in_=x[:, :, px, :])
            st["x_raw", g] = xr
            wr = raw.tile([P, 2, n, 4, F], BF16, name="w_raw%d" % g)
            nc.sync.dma_start(out=wr[:, 0], in_=w_dram[0][:, px])
            nc.sync.dma_start(out=wr[:, 1], in_=w_dram[1][:, px])
            st["w_raw", g] = wr

        def transposes(g):
            n = GROUPS[g]
            words = st["x_raw", g][:].rearrange("b r q c -> b (r q c)").bitcast(F32)
            banks = []
            for h in range(n):
                xt = pt.tile([P, 2, 2, B], F32, name="xt", tag="xt")
                for r in range(2):
                    s = r * n + h
                    for u in range(2):
                        nc.tensor.transpose(xt[:, r, u, :], words[:, 256 * s + u : 256 * (s + 1) : 2], ident[:])
                banks.append(xt)
            st["xt", g] = banks

        def x_copies(g, eng):
            n = GROUPS[g]
            if ("xg", g) not in st:
                st["xg", g] = grp.tile([P, 2 * n, B, 4], BF16, name="xg", tag="xg", align_bytes=64)
            xg_w = st["xg", g][:].rearrange("p s b t -> p (s b t)").bitcast(F32).rearrange("p (s b u) -> p s b u", s=2 * n, u=2)
            for h in range(n):
                src = st["xt", g][h][:].rearrange("p i u b -> p i b u")
                on_v = h >= n - V_BANKS[g]
                if on_v and eng == "v":
                    nc.vector.tensor_copy(out=xg_w[:, 2 * h : 2 * h + 2], in_=src)
                if not on_v and eng == "s":
                    nc.scalar.copy(out=xg_w[:, 2 * h : 2 * h + 2], in_=src)

        def wg_of(g):
            if ("wg", g) not in st:
                st["wg", g] = grp.tile([P, 2 * GROUPS[g], F, 4], BF16, name="wg", tag="wg", align_bytes=64, bufs=1)
            return st["wg", g]

        def w_copies(g, letter):
            for lo, hi in runs(w_plan(g), letter):
                wg = wg_of(g)
                slots = st["w_raw", g][:].rearrange("p w q j f -> p (w q) j f")
                blk = G_BLOCK if letter == "g" else BLOCK
                blk_dst = wg[:, lo:hi].rearrange("p s (c i) j -> p s c j i", i=max(blk, 1))
                blk_src = slots[:, lo:hi].rearrange("p s j (c i) -> p s c j i", i=max(blk, 1))
                if letter == "s":
                    nc.scalar.copy(out=blk_dst, in_=blk_src)
                elif letter == "v":
                    nc.vector.tensor_copy(out=blk_dst, in_=blk_src)
                elif blk > 0:
                    nc.gpsimd.tensor_scalar(out=blk_dst, in0=blk_src, scalar1=1.0, scalar2=0.0, op0=ALU.mult, op1=ALU.add)
                else:
                    nc.gpsimd.tensor_scalar(
                        out=wg[:, lo:hi], in0=slots[:, lo:hi].rearrange("p s j f -> p s f j"), scalar1=1.0, scalar2=0.0, op0=ALU.mult, op1=ALU.add
                    )

        def w_p_mm(g):
            slots = st["w_raw", g][:].rearrange("p w q j f -> p (w q) j f")
            for lo, hi in runs(w_plan(g), "p"):
                assert hi - lo == 2
                wp = pt.tile([P, 2, F, 4], BF16, name="wp", tag="wp", bufs=1)
                for h in range(2):
                    nc.tensor.matmul(out=wp[:, h], lhsT=ident_bf[:], rhs=slots[:, lo + h].rearrange("p j f -> p f j"), start=True, stop=True)
                st["wp", g, lo] = wp

        def w_p_copy(g):
            for lo, hi in runs(w_plan(g), "p"):
                nc.scalar.copy(out=wg_of(g)[:, lo:hi], in_=st["wp", g, lo][:])

        def quant_x(g):
            n = GROUPS[g]
            xc = code.tile([P, 2 * n * B], U32, name="xc", tag="xc", align_bytes=64)
            xs = code.tile([P, 2 * n * B], U8, name="xs", tag="xs", align_bytes=64)
            nc.vector.quantize_mx(out=xc[:].bitcast(FP8X4), scales=xs[:], in_=st["xg", g][:].rearrange("p s b t -> p (s b t)"))
            st["qx", g] = (xc, xs)

        def quant_w(g):
            n = GROUPS[g]
            wc = code.tile([P, 2 * n * F], U32, name="wc", tag="wc", align_bytes=64)
            ws = code.tile([P, 2 * n * F], U8, name="ws", tag="ws", align_bytes=64)
            nc.vector.quantize_mx(out=wc[:].bitcast(FP8X4), scales=ws[:], in_=st["wg", g][:].rearrange("p s f t -> p (s f t)"))
            st["qw", g] = (wc, ws)

        def products(g):
            n = GROUPS[g]
            xc, xs = st["qx", g]
            wc, ws = st["qw", g]
            acc_rr = pa.tile([P, n, F], F32, name="acc_rr", tag="acc_rr")
            if n <= MERGE_MAX:
                both = pa.tile([P, 2, n, F], F32, name="acc_both", tag="acc_im")
                acc_im, acc_ii = both[:, 0], both[:, 1]
                st["acc", g] = (acc_rr, both)
            else:
                im = pa.tile([P, n, F], F32, name="acc_im", tag="acc_im")
                ii = pa.tile([P, n, F], F32, name="acc_ii", tag="acc_ii")
                acc_im, acc_ii = im[:], ii[:]
                st["acc", g] = (acc_rr, im, ii)

            def mm(out, sx, sw, start, stop):
                cx = slice(B * sx, B * (sx + 1))
                cw = slice(F * sw, F * (sw + 1))
                nc.tensor.matmul_mx(
                    out=out,
                    lhsT=xc[:, cx].bitcast(FP8X4),
                    lhsT_scale=xs[:, cx],
                    rhs=wc[:, cw].bitcast(FP8X4),
                    rhs_scale=ws[:, cw],
                    start=start,
                    stop=stop,
                )

            for q in range(n):
                mm(acc_ii[:, q, :], 2 * q + 1, n + q, True, True)
            for q in range(n):
                mm(acc_im[:, q, :], 2 * q + 1, q, True, False)
                mm(acc_im[:, q, :], 2 * q, n + q, False, True)
            for q in range(n):
                mm(acc_rr[:, q, :], 2 * q, q, True, True)

        def sums_a(g):
            n = GROUPS[g]
            y = epi.tile([P, 3, n, F], F32, name="y", tag="y")
            acc = st["acc", g]
            if n <= MERGE_MAX:
                nc.vector.tensor_tensor(
                    out=y[:, 1:3], in0=acc[1][:], in1=bias[:].rearrange("p (k o) f -> p k o f", o=1).to_broadcast([P, 2, n, F]), op=ALU.add
                )
            else:
                nc.vector.tensor_tensor(out=y[:, 2], in0=acc[2][:], in1=bias[:, 1:2, :].to_broadcast([P, n, F]), op=ALU.add)
            st["y", g] = y

        def sums_b(g):
            n = GROUPS[g]
            y = st["y", g]
            acc = st["acc", g]
            if n > MERGE_MAX:
                nc.vector.tensor_tensor(out=y[:, 1], in0=acc[1][:], in1=bias[:, 0:1, :].to_broadcast([P, n, F]), op=ALU.add)
            nc.vector.tensor_tensor(out=y[:, 0], in0=acc[0][:], in1=y[:, 2], op=ALU.subtract)

        def res_of(g):
            c, off = chunk_of(RES_CHUNKS, first[g])
            if ("res", c) not in st:
                st["res", c] = epi.tile([P, 2, RES_CHUNKS[c], F], F32, name="res", tag="res", bufs=RES_BUFS)
            return st["res", c], off

        def relu(g, eng):
            n = GROUPS[g]
            plan = relu_plan(g)
            parts = [r for r in range(2) if plan[r] == eng]
            if not parts:
                return
            res, off = res_of(g)
            lo, hi = parts[0], parts[-1] + 1
            dst = res[:, lo:hi, off : off + n, :]
            src = st["y", g][:, lo:hi]
            if eng == "s":
                nc.scalar.activation(out=dst, in_=src, func=ACT.Relu)
            elif eng == "v":
                nc.vector.tensor_scalar(out=dst, in0=src, scalar1=0.0, scalar2=None, op0=ALU.max)
            else:
                nc.gpsimd.tensor_scalar(out=dst, in0=src, scalar1=FLT_MAX, scalar2=0.0, op0=ALU.min, op1=ALU.max)

        def store_res(g):
            n = GROUPS[g]
            c, off = chunk_of(RES_CHUNKS, first[g])
            m = RES_CHUNKS[c]
            if off + n == m:
                nc.sync.dma_start(out=o0[:, :, first[g] + n - m : first[g] + n, :], in_=st["res", c][:])

        def row_max(g):
            n = GROUPS[g]
            amax = sml.tile([P, 2 * n], F32, name="amax", tag="amax")
            nc.vector.tensor_reduce(out=amax[:], in_=st["y", g][:, 0:2].rearrange("p r q f -> p (r q) f"), axis=AX.X, op=ALU.max)
            st["amax", g] = amax

        def row_rcp(g):
            rcp = sml.tile([P, 2 * GROUPS[g]], F32, name="rcp", tag="rcp")
            nc.vector.reciprocal(out=rcp[:], in_=st["amax", g][:])
            st["rcp", g] = rcp

        def row_fac(g):
            fac = sml.tile([P, 2 * GROUPS[g]], F32, name="fac", tag="fac")
            nc.scalar.activation(out=fac[:], in_=st["rcp", g][:], func=ACT.Copy, scale=448.0)
            st["fac", g] = fac

        def casts(g, r):
            n = GROUPS[g]
            fac = st["fac", g]
            res, off = res_of(g)
            cb, offb = chunk_of(BYTE_CHUNKS, first[g])
            mb = BYTE_CHUNKS[cb]
            if ("byt", cb) not in st:
                st["byt", cb] = const.tile([P, 2, mb, F], FP8, name="byt%d" % cb)
            byt = st["byt", cb]
            for q in range(n):
                s = r * n + q
                if g == N - 1 and q < TAIL_V_CASTS:
                    nc.vector.tensor_scalar(
                        out=byt[:, r, offb + q, :], in0=res[:, r, off + q, :], scalar1=fac[:, s : s + 1], scalar2=None, op0=ALU.mult, saturate=False
                    )
                else:
                    nc.scalar.activation(
                        out=byt[:, r, offb + q, :], in_=res[:, r, off + q, :], func=ACT.Identity, scale=fac[:, s : s + 1], bias=zero[:, 0:1], saturate=False
                    )
            if offb + n == mb:
                nc.sync.dma_start(out=o1[:, r, first[g] + n - mb : first[g] + n, :], in_=byt[:, r].bitcast(U8))

        def load_bias():
            nc.sync.dma_start(out=brow[0:1, 0:F], in_=b_i.rearrange("(o f) -> o f", o=1))
            nc.sync.dma_start(out=brow[0:1, F : 2 * F], in_=b_r.rearrange("(o f) -> o f", o=1))

        def spread_bias():
            bp = pt.tile([P, 2, F], F32, name="bp", tag="xt")
            nc.tensor.matmul(out=bp[:].rearrange("p r f -> p (r f)"), lhsT=ones[:], rhs=brow[:], start=True, stop=True)
            nc.vector.tensor_copy(out=bias[:, 0], in_=bp[:, 0])
            nc.vector.tensor_scalar(out=bias[:, 1], in0=bp[:, 1], scalar1=-1.0, scalar2=None, op0=ALU.mult)

        stages = {
            "load": load,
            "transposes": transposes,
            "x_s": lambda g: x_copies(g, "s"),
            "x_v": lambda g: x_copies(g, "v"),
            "w_g": lambda g: w_copies(g, "g"),
            "w_s": lambda g: w_copies(g, "s"),
            "w_v": lambda g: w_copies(g, "v"),
            "w_p_mm": w_p_mm,
            "w_p_copy": w_p_copy,
            "quant_x": quant_x,
            "quant_w": quant_w,
            "products": products,
            "sums_a": sums_a,
            "sums_b": sums_b,
            "row_max": row_max,
            "row_rcp": row_rcp,
            "row_fac": row_fac,
            "relu_s": lambda g: relu(g, "s"),
            "relu_v": lambda g: relu(g, "v"),
            "relu_g": lambda g: relu(g, "g"),
            "store_res": store_res,
            "casts_soon": lambda g: [casts(g, r) for r in (1, 0) if relu_plan(g)[r] != "g"],
            "casts_late": lambda g: [casts(g, r) for r in (1, 0) if relu_plan(g)[r] == "g"],
        }

        brow = const.tile([P, 2 * F], BF16, name="brow")
        nc.gpsimd.memset(brow[:], 0.0)
        for g in range(LOADS_FIRST + 1):
            if g == BIAS_LOAD_AFTER:
                load_bias()
            if g < LOADS_FIRST:
                load(g)
        zero = const.tile([P, 1], F32, name="zero")
        nc.vector.memset(zero[:], 0.0)
        warm = const.tile([P, 1], F32, name="warm")
        nc.scalar.activation(out=warm[:], in_=zero[:], func=ACT.Relu)
        ident = const.tile([P, P], F32, name="ident")
        make_identity(nc, ident[:])
        ones = const.tile([P, P], BF16, name="ones")
        nc.vector.memset(ones[:], 1.0)
        bias = const.tile([P, 2, F], F32, name="bias")
        if any("p" in plan for plan in W_PLAN.values()):
            ident_bf = const.tile([P, P], BF16, name="ident_bf")
            make_identity(nc, ident_bf[:])

        if BIAS_AT <= -9:
            spread_bias()
        lags = [lag for name, lag in ORDER]
        for i in range(-max(lags), N - min(lags)):
            for name, lag in ORDER:
                g = i + lag
                if name == "load" and g < LOADS_FIRST:
                    continue
                if name == "sums_a" and g == 0 and BIAS_AT > -9:
                    nc.vector.tensor_copy(out=bias[:, 0], in_=st["bp", 0][:, 0])
                    nc.vector.tensor_scalar(out=bias[:, 1], in0=st["bp", 0][:, 1], scalar1=-1.0, scalar2=None, op0=ALU.mult)
                if 0 <= g < N:
                    stages[name](g)
                if name == "transposes" and i == BIAS_AT:
                    bp = pt.tile([P, 2, F], F32, name="bp", tag="xt")
                    nc.tensor.matmul(out=bp[:].rearrange("p r f -> p (r f)"), lhsT=ones[:], rhs=brow[:], start=True, stop=True)
                    st["bp", 0] = bp
